import numpy as np
import ml_dtypes


def mxq(x, axis, fmt="e4m3"):
    dtype, down = {"e4m3": (ml_dtypes.float8_e4m3fn, 7), "e5m2": (ml_dtypes.float8_e5m2, 14)}[fmt]
    v = np.moveaxis(np.asarray(x, np.float32).astype(ml_dtypes.bfloat16).astype(np.float64), axis, -1)
    blocks = v.reshape(v.shape[:-1] + (-1, 32))
    amax = np.abs(blocks).max(-1, keepdims=True)
    byte = np.maximum(np.where(amax > 0, np.frexp(amax)[1] - 1 + 127, 0) - down, 1)
    scale = np.exp2(byte - 127.0)
    codes = (blocks / scale).astype(np.float32).astype(dtype).astype(np.float64)
    return np.moveaxis((codes * scale).reshape(v.shape), -1, axis)


WIDE = False


def mx_kscale(k):
    if not WIDE:
        return np.ones(k)
    levels = np.array([10, -10, 5, -5, 0])
    a = np.random.permutation(np.resize(levels, k // 512 * 4)).reshape(k // 512, 4)
    idx = np.arange(k)
    return np.exp2(a[idx // 512, idx % 128 // 32])


BF16 = ml_dtypes.bfloat16


def bf(x):
    return np.asarray(x, np.float32).astype(BF16)


def f64(x):
    return np.asarray(x).astype(np.float64)


B, T, I, H = 128, 8, 1024, 1024


def sigmoid(v):
    return 1.0 / (1.0 + np.exp(-v))


def setup_inputs():
    s = mx_kscale(I)
    d = {"x": bf(np.random.standard_normal((B, T, I)) * s),
         "h0": bf(np.random.standard_normal((B, H))),
         "c0": bf(np.random.standard_normal((B, H)))}
    for n in ("f", "i", "g"):
        d["W_" + n] = bf(np.random.standard_normal((H, I)) / np.sqrt(I) / s)
        d["b_" + n] = bf(np.random.standard_normal(H) * 0.5)
        d["R_" + n] = bf(np.random.standard_normal((H, H)) / np.sqrt(H))
        d["rb_" + n] = bf(np.random.standard_normal(H) * 0.5)
    return d


def reference(x, h0, c0, W_f, b_f, R_f, rb_f, W_i, b_i, R_i, rb_i, W_g, b_g, R_g, rb_g):
    xq = mxq(f64(x), 2, "e4m3")
    h0v = f64(h0)

    def pre(W, b, R, rb):
        return (xq @ mxq(f64(W), 1, "e4m3").T) + f64(b) + (h0v @ f64(R).T + f64(rb))[:, None, :]

    ft = sigmoid(pre(W_f, b_f, R_f, rb_f))
    it = sigmoid(pre(W_i, b_i, R_i, rb_i))
    gt = np.tanh(pre(W_g, b_g, R_g, rb_g))
    c = ft * f64(c0)[:, None, :] + it * gt
    h_seq = np.tanh(c)
    hidden_seq = np.transpose(h_seq, (1, 0, 2)).reshape(T * B, H).T
    return (hidden_seq, h_seq[:, -1, :], c[:, -1, :])

@@ -1,0 +1,272 @@
+from contextlib import ExitStack
+
+import concourse.mybir as mybir
+from concourse.masks import make_identity
+
+F32 = mybir.dt.float32
+BF16 = mybir.dt.bfloat16
+U32 = mybir.dt.uint32
+U8 = mybir.dt.uint8
+FP8X4 = mybir.dt.float8_e4m3fn_x4
+ACT = mybir.ActivationFunctionType
+ALU = mybir.AluOpType
+
+P = 128
+BATCH, STEPS, FEATURES, HIDDEN = 128, 8, 1024, 1024
+GATES = 3
+ROW_TILES = HIDDEN // P
+WORD_BLOCKS = FEATURES // (2 * P)
+PASSES = FEATURES // (4 * P)
+HALF_STEPS = STEPS // 2
+HALF = HALF_STEPS * BATCH
+TOKENS = STEPS * BATCH
+
+FLOPS = 2 * TOKENS * FEATURES * HIDDEN * GATES + 2 * BATCH * HIDDEN * HIDDEN * GATES
+
+
+def tile_lstm_cell_pa_kernel(
+    tc, x, h0, c0, W_f, b_f, R_f, rb_f, W_i, b_i, R_i, rb_i, W_g, b_g, R_g, rb_g, out_0, out_1, out_2
+):
+    nc = tc.nc
+    w_dram = (W_f, W_i, W_g)
+    r_dram = (R_f, R_i, R_g)
+    bias_dram = (b_f, rb_f, b_i, rb_i, b_g, rb_g)
+    gate_func = (ACT.Sigmoid, ACT.Sigmoid, ACT.Tanh)
+
+    with ExitStack() as ctx:
+        const = ctx.enter_context(tc.tile_pool(name="const", bufs=1))
+        raw_pool = ctx.enter_context(tc.tile_pool(name="raw", bufs=18))
+        stage = ctx.enter_context(tc.tile_pool(name="stage", bufs=6))
+        work = ctx.enter_context(tc.tile_pool(name="work", bufs=3))
+        keep = ctx.enter_context(tc.tile_pool(name="keep", bufs=ROW_TILES))
+        flip_psum = ctx.enter_context(tc.psum_pool(name="flip_psum", bufs=3))
+        rec_psum = ctx.enter_context(tc.psum_pool(name="rec_psum", bufs=1))
+        acc_psum = ctx.enter_context(tc.psum_pool(name="acc_psum", bufs=4))
+
+        ident_f32 = const.tile([P, P], F32)
+        make_identity(nc, ident_f32[:])
+        ident_bf16 = const.tile([P, P], BF16)
+        make_identity(nc, ident_bf16[:])
+
+        table_warmer = const.tile([P, 1], F32)
+        nc.vector.memset(table_warmer[:], 0.0)
+        nc.scalar.activation(out=table_warmer[:], in_=table_warmer[:], func=ACT.Sigmoid)
+
+        x_raw = const.tile([P, STEPS, FEATURES], BF16)
+        h0_raw = const.tile([P, HIDDEN], BF16)
+        c0_raw = const.tile([P, HIDDEN], BF16)
+
+        def load_x(first_step):
+            steps = slice(first_step, first_step + 2)
+            nc.sync.dma_start(out=x_raw[:, steps, :], in_=x[:, steps, :])
+
+        def load_rows(matrix, jt, name):
+            raw = raw_pool.tile([P, FEATURES], BF16, tag="raw", name=name)
+            nc.sync.dma_start(out=raw[:], in_=matrix[jt * P : (jt + 1) * P, :])
+            return raw
+
+        def load_row_tile(jt):
+            r_raw = [load_rows(r_dram[n], jt, "r_raw") for n in range(GATES)]
+            w_raw = [load_rows(w_dram[n], jt, "w_raw") for n in range(GATES)]
+            return r_raw, w_raw
+
+        load_x(4)
+        load_x(6)
+        nc.sync.dma_start(out=h0_raw[:], in_=h0)
+        raw_tiles = {0: load_row_tile(0)}
+        nc.sync.dma_start(out=c0_raw[:], in_=c0)
+        load_x(0)
+        load_x(2)
+        raw_tiles[1] = load_row_tile(1)
+
+        bias_rows = const.tile([P, P], BF16)
+        nc.vector.memset(bias_rows[:], 0.0)
+        for v, vector in enumerate(bias_dram):
+            nc.scalar.dma_start(
+                out=bias_rows[v * ROW_TILES : (v + 1) * ROW_TILES, :],
+                in_=vector.rearrange("(jt p) -> jt p", p=P),
+            )
+
+        def transpose_words(rows_bf16):
+            words = rows_bf16.bitcast(F32)
+            bank = flip_psum.tile([P, WORD_BLOCKS, P], F32, tag="flip", name="bank")
+            for q in range(WORD_BLOCKS):
+                nc.tensor.transpose(bank[:, q, :], words[:, q * P : (q + 1) * P], ident_f32[:])
+            return bank
+
+        def by_pass(bank):
+            return bank[:].rearrange("p (c u) n -> p c n u", u=2)
+
+        x_grouped = const.tile([P, PASSES, 4 * TOKENS], BF16, align_bytes=64)
+        x_codes = const.tile([P, PASSES, TOKENS], U32, align_bytes=64)
+        x_scales = const.tile([P, PASSES, TOKENS], U8, align_bytes=64)
+        x_grouped_words = x_grouped[:].bitcast(F32).rearrange("p c (n u) -> p c n u", u=2)
+
+        def prepare_x(half):
+            for t in range(half * HALF_STEPS, (half + 1) * HALF_STEPS):
+                bank = transpose_words(x_raw[:, t, :])
+                columns = x_grouped_words[:, :, t * BATCH : (t + 1) * BATCH, :]
+                if t % 2 == 0:
+                    nc.scalar.copy(out=columns, in_=by_pass(bank))
+                else:
+                    nc.vector.tensor_copy(out=columns, in_=by_pass(bank))
+            for c in range(PASSES):
+                nc.vector.quantize_mx(
+                    out=x_codes[:, c, half * HALF : (half + 1) * HALF].bitcast(FP8X4),
+                    scales=x_scales[:, c, half * HALF : (half + 1) * HALF],
+                    in_=x_grouped[:, c, half * 4 * HALF : (half + 1) * 4 * HALF],
+                )
+
+        h0T = const.tile([P, WORD_BLOCKS, BATCH, 2], BF16)
+
+        def prepare_h0():
+            bank = transpose_words(h0_raw[:])
+            nc.vector.tensor_copy(
+                out=h0T[:].rearrange("p q b e -> p (q b e)").bitcast(F32),
+                in_=bank[:].rearrange("p q b -> p (q b)"),
+            )
+
+        def transpose_r(r_raw):
+            r_T = []
+            for n in range(GATES):
+                bank = transpose_words(r_raw[n][:])
+                flipped = stage.tile([P, WORD_BLOCKS, P, 2], BF16, tag="r_T", name="r_T")
+                nc.vector.tensor_copy(
+                    out=flipped[:].rearrange("p q j e -> p (q j e)").bitcast(F32),
+                    in_=bank[:].rearrange("p q j -> p (q j)"),
+                )
+                r_T.append(flipped)
+            return r_T
+
+        def recurrent(r_T):
+            sums = rec_psum.tile([P, GATES, BATCH], F32, tag="rec", name="rec_sums")
+            for n in range(GATES):
+                for q in range(WORD_BLOCKS):
+                    for e in range(2):
+                        nc.tensor.matmul(
+                            out=sums[:, n, :],
+                            lhsT=r_T[n][:, q, :, e],
+                            rhs=h0T[:, q, :, e],
+                            start=(q == 0 and e == 0),
+                            stop=(q == WORD_BLOCKS - 1 and e == 1),
+                        )
+            rec = work.tile([P, GATES, BATCH], F32, tag="rec_sb", name="rec")
+            nc.scalar.copy(out=rec[:], in_=sums[:])
+            return rec
+
+        def quantise_w(w_raw):
+            grouped = []
+            for n in range(GATES):
+                bank = transpose_words(w_raw[n][:])
+                values = stage.tile([P, 4 * PASSES * P], BF16, tag="w_grouped", name="w_grouped", align_bytes=64)
+                nc.scalar.copy(
+                    out=values[:].bitcast(F32).rearrange("p (c j u) -> p c j u", c=PASSES, u=2),
+                    in_=by_pass(bank),
+                )
+                grouped.append(values)
+            w_mx = []
+            for n in range(GATES):
+                codes = stage.tile([P, PASSES, P], U32, tag="w_codes", name="w_codes", align_bytes=64)
+                scales = stage.tile([P, PASSES, P], U8, tag="w_scales", name="w_scales", align_bytes=64)
+                nc.vector.quantize_mx(
+                    out=codes[:].rearrange("p c j -> p (c j)").bitcast(FP8X4),
+                    scales=scales[:].rearrange("p c j -> p (c j)"),
+                    in_=grouped[n][:],
+                )
+                w_mx.append((codes, scales))
+            return w_mx
+
+        def gates(jt, half, w_mx, rec):
+            tokens = slice(half * HALF, (half + 1) * HALF)
+            out = []
+            for n in range(GATES):
+                codes, scales = w_mx[n]
+                acc = acc_psum.tile([P, HALF_STEPS, BATCH], F32, tag="acc", name="acc")
+                for c in range(PASSES):
+                    nc.tensor.matmul_mx(
+                        out=acc[:].rearrange("p t b -> p (t b)"),
+                        lhsT=codes[:, c, :].bitcast(FP8X4),
+                        lhsT_scale=scales[:, c, :],
+                        rhs=x_codes[:, c, tokens].bitcast(FP8X4),
+                        rhs_scale=x_scales[:, c, tokens],
+                        start=(c == 0),
+                        stop=(c == PASSES - 1),
+                    )
+                gate = work.tile([P, HALF_STEPS, BATCH], F32, tag="gate%d" % n, name="gate")
+                nc.vector.tensor_tensor(
+                    out=gate[:],
+                    in0=acc[:],
+                    in1=rec[:, n, :].unsqueeze(1).to_broadcast([P, HALF_STEPS, BATCH]),
+                    op=ALU.add,
+                )
+                nc.scalar.activation(out=gate[:], in_=gate[:], func=gate_func[n], bias=bias[:, n, jt : jt + 1])
+                out.append(gate)
+            return out
+
+        def cell(jt, half, gate_tiles):
+            f_gate, i_gate, g_gate = gate_tiles
+            pool = keep if half == 1 else work
+            nc.gpsimd.tensor_tensor(
+                out=f_gate[:],
+                in0=f_gate[:],
+                in1=c0T[:, jt, :].unsqueeze(1).to_broadcast([P, HALF_STEPS, BATCH]),
+                op=ALU.mult,
+            )
+            nc.gpsimd.tensor_tensor(out=i_gate[:], in0=i_gate[:], in1=g_gate[:], op=ALU.mult)
+            c_new = pool.tile([P, HALF_STEPS, BATCH], F32, tag="c_new", name="c_new")
+            nc.vector.tensor_tensor(out=c_new[:], in0=f_gate[:], in1=i_gate[:], op=ALU.add)
+            h_new = pool.tile([P, HALF_STEPS, BATCH], F32, tag="h_new", name="h_new")
+            nc.scalar.activation(out=h_new[:], in_=c_new[:], func=ACT.Tanh)
+            nc.sync.dma_start(
+                out=out_0[jt * P : (jt + 1) * P, half * HALF : (half + 1) * HALF],
+                in_=h_new[:].rearrange("p t b -> p (t b)"),
+            )
+            return h_new, c_new
+
+        prepare_x(1)
+        prepare_h0()
+        r_T = transpose_r(raw_tiles[0][0])
+        rec = recurrent(r_T)
+        w_mx = quantise_w(raw_tiles[0][1])
+
+        bias_psum = flip_psum.tile([P, P], BF16, tag="flip", name="bias_psum")
+        nc.tensor.transpose(bias_psum[:], bias_rows[:], ident_bf16[:])
+        bias_pairs = const.tile([P, GATES, 2, ROW_TILES], F32)
+        nc.vector.tensor_copy(
+            out=bias_pairs[:],
+            in_=bias_psum[:, 0 : 2 * GATES * ROW_TILES].rearrange("p (n s jt) -> p n s jt", n=GATES, s=2),
+        )
+        bias = const.tile([P, GATES, ROW_TILES], F32)
+        nc.vector.tensor_tensor(out=bias[:], in0=bias_pairs[:, :, 0, :], in1=bias_pairs[:, :, 1, :], op=ALU.add)
+
+        c0_psum = flip_psum.tile([P, ROW_TILES, BATCH], BF16, tag="flip", name="c0_psum")
+        for jt in range(ROW_TILES):
+            nc.tensor.transpose(c0_psum[:, jt, :], c0_raw[:, jt * P : (jt + 1) * P], ident_bf16[:])
+        c0T = const.tile([P, ROW_TILES, BATCH], F32)
+        nc.scalar.copy(out=c0T[:], in_=c0_psum[:])
+
+        last_tiles = []
+        for jt in range(ROW_TILES):
+            if jt + 2 < ROW_TILES:
+                raw_tiles[jt + 2] = load_row_tile(jt + 2)
+            late_gates = gates(jt, 1, w_mx, rec)
+            if jt == 0:
+                prepare_x(0)
+            if jt + 1 < ROW_TILES:
+                r_T = transpose_r(raw_tiles[jt + 1][0])
+            last_tiles.append(cell(jt, 1, late_gates))
+            early_gates = gates(jt, 0, w_mx, rec)
+            if jt + 1 < ROW_TILES:
+                w_mx = quantise_w(raw_tiles[jt + 1][1])
+                rec = recurrent(r_T)
+            cell(jt, 0, early_gates)
+
+        last_sb = const.tile([P, 2, HIDDEN], F32)
+        for first in range(0, ROW_TILES, WORD_BLOCKS):
+            columns = slice(first * P, (first + WORD_BLOCKS) * P)
+            for which, out_last in enumerate((out_1, out_2)):
+                bank = flip_psum.tile([P, WORD_BLOCKS, P], F32, tag="flip", name="last_bank")
+                for q in range(WORD_BLOCKS):
+                    nc.tensor.transpose(bank[:, q, :], last_tiles[first + q][which][:, HALF_STEPS - 1, :], ident_f32[:])
+                nc.vector.tensor_copy(out=last_sb[:, which, columns], in_=bank[:].rearrange("p q j -> p (q j)"))
+                nc.sync.dma_start(out=out_last[:, columns], in_=last_sb[:, which, columns])

@@ -20,6 +20,7 @@ PASSES = FEATURES // (4 * P)
 HALF_STEPS = STEPS // 2
 HALF = HALF_STEPS * BATCH
 TOKENS = STEPS * BATCH
+LOAD_AHEAD = 3
 
 FLOPS = 2 * TOKENS * FEATURES * HIDDEN * GATES + 2 * BATCH * HIDDEN * HIDDEN * GATES
 
@@ -35,7 +36,7 @@ def tile_lstm_cell_pa_kernel(
 
     with ExitStack() as ctx:
         const = ctx.enter_context(tc.tile_pool(name="const", bufs=1))
-        raw_pool = ctx.enter_context(tc.tile_pool(name="raw", bufs=18))
+        raw_pool = ctx.enter_context(tc.tile_pool(name="raw", bufs=2 * GATES * (LOAD_AHEAD + 1)))
         stage = ctx.enter_context(tc.tile_pool(name="stage", bufs=6))
         work = ctx.enter_context(tc.tile_pool(name="work", bufs=3))
         keep = ctx.enter_context(tc.tile_pool(name="keep", bufs=ROW_TILES))
@@ -43,10 +44,20 @@ def tile_lstm_cell_pa_kernel(
         rec_psum = ctx.enter_context(tc.psum_pool(name="rec_psum", bufs=1))
         acc_psum = ctx.enter_context(tc.psum_pool(name="acc_psum", bufs=4))
 
+        ctx.enter_context(tc.manual_schedule())
+
         ident_f32 = const.tile([P, P], F32)
         make_identity(nc, ident_f32[:])
         ident_bf16 = const.tile([P, P], BF16)
         make_identity(nc, ident_bf16[:])
+
+        bias_rows = const.tile([P, P], BF16)
+        nc.vector.memset(bias_rows[:], 0.0)
+        for v, vector in enumerate(bias_dram):
+            nc.scalar.dma_start(
+                out=bias_rows[v * ROW_TILES : (v + 1) * ROW_TILES, :],
+                in_=vector.rearrange("(jt p) -> jt p", p=P),
+            )
 
         table_warmer = const.tile([P, 1], F32)
         nc.vector.memset(table_warmer[:], 0.0)
@@ -66,26 +77,20 @@ def tile_lstm_cell_pa_kernel(
             return raw
 
         def load_row_tile(jt):
-            r_raw = [load_rows(r_dram[n], jt, "r_raw") for n in range(GATES)]
-            w_raw = [load_rows(w_dram[n], jt, "w_raw") for n in range(GATES)]
-            return r_raw, w_raw
+            r_raw[jt] = [load_rows(r_dram[n], jt, "r_raw") for n in range(GATES)]
+            w_raw[jt] = [load_rows(w_dram[n], jt, "w_raw") for n in range(GATES)]
 
+        r_raw = {}
+        w_raw = {}
         load_x(4)
         load_x(6)
         nc.sync.dma_start(out=h0_raw[:], in_=h0)
-        raw_tiles = {0: load_row_tile(0)}
+        load_row_tile(0)
         nc.sync.dma_start(out=c0_raw[:], in_=c0)
         load_x(0)
         load_x(2)
-        raw_tiles[1] = load_row_tile(1)
-
-        bias_rows = const.tile([P, P], BF16)
-        nc.vector.memset(bias_rows[:], 0.0)
-        for v, vector in enumerate(bias_dram):
-            nc.scalar.dma_start(
-                out=bias_rows[v * ROW_TILES : (v + 1) * ROW_TILES, :],
-                in_=vector.rearrange("(jt p) -> jt p", p=P),
-            )
+        for jt in range(1, LOAD_AHEAD):
+            load_row_tile(jt)
 
         def transpose_words(rows_bf16):
             words = rows_bf16.bitcast(F32)
@@ -96,6 +101,12 @@ def tile_lstm_cell_pa_kernel(
 
         def by_pass(bank):
             return bank[:].rearrange("p (c u) n -> p c n u", u=2)
+
+        def leave_psum(n, out, in_):
+            if n % GATES == 1:
+                nc.vector.tensor_copy(out=out, in_=in_)
+            else:
+                nc.scalar.copy(out=out, in_=in_)
 
         x_grouped = const.tile([P, PASSES, 4 * TOKENS], BF16, align_bytes=64)
         x_codes = const.tile([P, PASSES, TOKENS], U32, align_bytes=64)
@@ -126,44 +137,50 @@ def tile_lstm_cell_pa_kernel(
                 in_=bank[:].rearrange("p q b -> p (q b)"),
             )
 
-        def transpose_r(r_raw):
+        def transpose_r(jt):
             r_T = []
             for n in range(GATES):
-                bank = transpose_words(r_raw[n][:])
+                bank = transpose_words(r_raw[jt][n][:])
                 flipped = stage.tile([P, WORD_BLOCKS, P, 2], BF16, tag="r_T", name="r_T")
-                nc.vector.tensor_copy(
+                leave_psum(
+                    n,
                     out=flipped[:].rearrange("p q j e -> p (q j e)").bitcast(F32),
                     in_=bank[:].rearrange("p q j -> p (q j)"),
                 )
                 r_T.append(flipped)
             return r_T
 
-        def recurrent(r_T):
-            sums = rec_psum.tile([P, GATES, BATCH], F32, tag="rec", name="rec_sums")
-            for n in range(GATES):
-                for q in range(WORD_BLOCKS):
-                    for e in range(2):
-                        nc.tensor.matmul(
-                            out=sums[:, n, :],
-                            lhsT=r_T[n][:, q, :, e],
-                            rhs=h0T[:, q, :, e],
-                            start=(q == 0 and e == 0),
-                            stop=(q == WORD_BLOCKS - 1 and e == 1),
-                        )
+        rec_steps = [(n, q, e) for n in range(GATES) for q in range(WORD_BLOCKS) for e in range(2)]
+
+        def recurrent_matmuls(sums, r_T, steps):
+            for n, q, e in steps:
+                nc.tensor.matmul(
+                    out=sums[:, n, :],
+                    lhsT=r_T[n][:, q, :, e],
+                    rhs=h0T[:, q, :, e],
+                    start=(q == 0 and e == 0),
+                    stop=(q == WORD_BLOCKS - 1 and e == 1),
+                )
+
+        def recurrent_out(sums):
             rec = work.tile([P, GATES, BATCH], F32, tag="rec_sb", name="rec")
             nc.scalar.copy(out=rec[:], in_=sums[:])
             return rec
 
-        def quantise_w(w_raw):
+        def transpose_w(jt):
             grouped = []
             for n in range(GATES):
-                bank = transpose_words(w_raw[n][:])
+                bank = transpose_words(w_raw[jt][n][:])
                 values = stage.tile([P, 4 * PASSES * P], BF16, tag="w_grouped", name="w_grouped", align_bytes=64)
-                nc.scalar.copy(
+                leave_psum(
+                    n,
                     out=values[:].bitcast(F32).rearrange("p (c j u) -> p c j u", c=PASSES, u=2),
                     in_=by_pass(bank),
                 )
                 grouped.append(values)
+            return grouped
+
+        def quantise_w(grouped):
             w_mx = []
             for n in range(GATES):
                 codes = stage.tile([P, PASSES, P], U32, tag="w_codes", name="w_codes", align_bytes=64)
@@ -178,7 +195,7 @@ def tile_lstm_cell_pa_kernel(
 
         def gates(jt, half, w_mx, rec):
             tokens = slice(half * HALF, (half + 1) * HALF)
-            out = []
+            gate_tiles = []
             for n in range(GATES):
                 codes, scales = w_mx[n]
                 acc = acc_psum.tile([P, HALF_STEPS, BATCH], F32, tag="acc", name="acc")
@@ -200,34 +217,52 @@ def tile_lstm_cell_pa_kernel(
                     op=ALU.add,
                 )
                 nc.scalar.activation(out=gate[:], in_=gate[:], func=gate_func[n], bias=bias[:, n, jt : jt + 1])
-                out.append(gate)
-            return out
+                gate_tiles.append(gate)
+            return gate_tiles
 
-        def cell(jt, half, gate_tiles):
+        def products(engine, jt, gate_tiles):
             f_gate, i_gate, g_gate = gate_tiles
-            pool = keep if half == 1 else work
-            nc.gpsimd.tensor_tensor(
+            engine.tensor_tensor(
                 out=f_gate[:],
                 in0=f_gate[:],
                 in1=c0T[:, jt, :].unsqueeze(1).to_broadcast([P, HALF_STEPS, BATCH]),
                 op=ALU.mult,
             )
-            nc.gpsimd.tensor_tensor(out=i_gate[:], in0=i_gate[:], in1=g_gate[:], op=ALU.mult)
+            engine.tensor_tensor(out=i_gate[:], in0=i_gate[:], in1=g_gate[:], op=ALU.mult)
+
+        def finish(jt, half, gate_tiles):
+            pool = keep if half == 1 else work
             c_new = pool.tile([P, HALF_STEPS, BATCH], F32, tag="c_new", name="c_new")
-            nc.vector.tensor_tensor(out=c_new[:], in0=f_gate[:], in1=i_gate[:], op=ALU.add)
+            nc.vector.tensor_tensor(out=c_new[:], in0=gate_tiles[0][:], in1=gate_tiles[1][:], op=ALU.add)
             h_new = pool.tile([P, HALF_STEPS, BATCH], F32, tag="h_new", name="h_new")
             nc.scalar.activation(out=h_new[:], in_=c_new[:], func=ACT.Tanh)
             nc.sync.dma_start(
                 out=out_0[jt * P : (jt + 1) * P, half * HALF : (half + 1) * HALF],
                 in_=h_new[:].rearrange("p t b -> p (t b)"),
             )
-            return h_new, c_new
+            if half == 1:
+                last_tiles[jt] = (h_new, c_new)
+
+        last_tiles = {}
+        last_sb = const.tile([P, 2, HIDDEN], F32)
+
+        def store_last(first):
+            columns = slice(first * P, (first + WORD_BLOCKS) * P)
+            for which, out_last in enumerate((out_1, out_2)):
+                bank = flip_psum.tile([P, WORD_BLOCKS, P], F32, tag="flip", name="last_bank")
+                for q in range(WORD_BLOCKS):
+                    nc.tensor.transpose(bank[:, q, :], last_tiles[first + q][which][:, HALF_STEPS - 1, :], ident_f32[:])
+                leave_psum(which, out=last_sb[:, which, columns], in_=bank[:].rearrange("p q j -> p (q j)"))
+                nc.sync.dma_start(out=out_last[:, columns], in_=last_sb[:, which, columns])
 
         prepare_x(1)
         prepare_h0()
-        r_T = transpose_r(raw_tiles[0][0])
-        rec = recurrent(r_T)
-        w_mx = quantise_w(raw_tiles[0][1])
+        r_T = transpose_r(0)
+        w_grouped = transpose_w(0)
+        rec_sums = rec_psum.tile([P, GATES, BATCH], F32, tag="rec", name="rec_sums")
+        recurrent_matmuls(rec_sums, r_T, rec_steps)
+        rec = recurrent_out(rec_sums)
+        w_mx = quantise_w(w_grouped)
 
         bias_psum = flip_psum.tile([P, P], BF16, tag="flip", name="bias_psum")
         nc.tensor.transpose(bias_psum[:], bias_rows[:], ident_bf16[:])
@@ -245,28 +280,37 @@ def tile_lstm_cell_pa_kernel(
         c0T = const.tile([P, ROW_TILES, BATCH], F32)
         nc.scalar.copy(out=c0T[:], in_=c0_psum[:])
 
-        last_tiles = []
-        for jt in range(ROW_TILES):
-            if jt + 2 < ROW_TILES:
-                raw_tiles[jt + 2] = load_row_tile(jt + 2)
-            late_gates = gates(jt, 1, w_mx, rec)
-            if jt == 0:
-                prepare_x(0)
-            if jt + 1 < ROW_TILES:
-                r_T = transpose_r(raw_tiles[jt + 1][0])
-            last_tiles.append(cell(jt, 1, late_gates))
-            early_gates = gates(jt, 0, w_mx, rec)
-            if jt + 1 < ROW_TILES:
-                w_mx = quantise_w(raw_tiles[jt + 1][1])
-                rec = recurrent(r_T)
-            cell(jt, 0, early_gates)
+        prepare_x(0)
+        r_T_next = transpose_r(1)
 
-        last_sb = const.tile([P, 2, HIDDEN], F32)
-        for first in range(0, ROW_TILES, WORD_BLOCKS):
-            columns = slice(first * P, (first + WORD_BLOCKS) * P)
-            for which, out_last in enumerate((out_1, out_2)):
-                bank = flip_psum.tile([P, WORD_BLOCKS, P], F32, tag="flip", name="last_bank")
-                for q in range(WORD_BLOCKS):
-                    nc.tensor.transpose(bank[:, q, :], last_tiles[first + q][which][:, HALF_STEPS - 1, :], ident_f32[:])
-                nc.vector.tensor_copy(out=last_sb[:, which, columns], in_=bank[:].rearrange("p q j -> p (q j)"))
-                nc.sync.dma_start(out=out_last[:, columns], in_=last_sb[:, which, columns])
+        unfinished = None
+        for jt in range(ROW_TILES):
+            if jt + LOAD_AHEAD < ROW_TILES:
+                load_row_tile(jt + LOAD_AHEAD)
+            more = jt + 1 < ROW_TILES
+            for half in (1, 0):
+                gate_tiles = gates(jt, half, w_mx, rec)
+                if half == 1 and more:
+                    w_grouped = transpose_w(jt + 1)
+                    rec_sums = rec_psum.tile([P, GATES, BATCH], F32, tag="rec", name="rec_sums")
+                    recurrent_matmuls(rec_sums, r_T_next, rec_steps[: len(rec_steps) // 2])
+                if half == 0 and more:
+                    r_T = r_T_next
+                    if jt + 2 < ROW_TILES:
+                        r_T_next = transpose_r(jt + 2)
+                    recurrent_matmuls(rec_sums, r_T, rec_steps[len(rec_steps) // 2 :])
+                    rec_next = recurrent_out(rec_sums)
+                if unfinished is not None:
+                    finish(*unfinished)
+                very_last = jt == ROW_TILES - 1 and half == 0
+                products(nc.vector if very_last else nc.gpsimd, jt, gate_tiles)
+                unfinished = (jt, half, gate_tiles)
+                if half == 1 and more:
+                    w_mx_next = quantise_w(w_grouped)
+            if more:
+                w_mx = w_mx_next
+                rec = rec_next
+            if jt == WORD_BLOCKS:
+                store_last(0)
+        store_last(WORD_BLOCKS)
+        finish(*unfinished)

@@ -36,13 +36,14 @@ def tile_lstm_cell_pa_kernel(
 
     with ExitStack() as ctx:
         const = ctx.enter_context(tc.tile_pool(name="const", bufs=1))
-        raw_pool = ctx.enter_context(tc.tile_pool(name="raw", bufs=2 * GATES * (LOAD_AHEAD + 1)))
+        raw_pool = ctx.enter_context(tc.tile_pool(name="raw", bufs=2 * GATES * LOAD_AHEAD))
         stage = ctx.enter_context(tc.tile_pool(name="stage", bufs=6))
         work = ctx.enter_context(tc.tile_pool(name="work", bufs=3))
         keep = ctx.enter_context(tc.tile_pool(name="keep", bufs=ROW_TILES))
         flip_psum = ctx.enter_context(tc.psum_pool(name="flip_psum", bufs=3))
         rec_psum = ctx.enter_context(tc.psum_pool(name="rec_psum", bufs=1))
-        acc_psum = ctx.enter_context(tc.psum_pool(name="acc_psum", bufs=4))
+        acc_psum = ctx.enter_context(tc.psum_pool(name="acc_psum", bufs=GATES))
+        c0_psum = ctx.enter_context(tc.psum_pool(name="c0_psum", bufs=1))
 
         ctx.enter_context(tc.manual_schedule())
 
@@ -137,8 +138,16 @@ def tile_lstm_cell_pa_kernel(
                 in_=bank[:].rearrange("p q b -> p (q b)"),
             )
 
+        r_T = {}
+        rec_sums = {}
+        rec = {}
+        w_grouped = {}
+        w_mx = {}
+
         def transpose_r(jt):
-            r_T = []
+            if jt >= ROW_TILES:
+                return
+            r_T[jt] = []
             for n in range(GATES):
                 bank = transpose_words(r_raw[jt][n][:])
                 flipped = stage.tile([P, WORD_BLOCKS, P, 2], BF16, tag="r_T", name="r_T")
@@ -147,28 +156,32 @@ def tile_lstm_cell_pa_kernel(
                     out=flipped[:].rearrange("p q j e -> p (q j e)").bitcast(F32),
                     in_=bank[:].rearrange("p q j -> p (q j)"),
                 )
-                r_T.append(flipped)
-            return r_T
+                r_T[jt].append(flipped)
 
         rec_steps = [(n, q, e) for n in range(GATES) for q in range(WORD_BLOCKS) for e in range(2)]
 
-        def recurrent_matmuls(sums, r_T, steps):
-            for n, q, e in steps:
+        def recurrent_matmuls(jt, part):
+            if jt >= ROW_TILES:
+                return
+            if part == 0:
+                rec_sums[jt] = rec_psum.tile([P, GATES, BATCH], F32, tag="rec", name="rec_sums")
+            count = len(rec_steps) // 2
+            for n, q, e in rec_steps[part * count : (part + 1) * count]:
                 nc.tensor.matmul(
-                    out=sums[:, n, :],
-                    lhsT=r_T[n][:, q, :, e],
+                    out=rec_sums[jt][:, n, :],
+                    lhsT=r_T[jt][n][:, q, :, e],
                     rhs=h0T[:, q, :, e],
                     start=(q == 0 and e == 0),
                     stop=(q == WORD_BLOCKS - 1 and e == 1),
                 )
-
-        def recurrent_out(sums):
-            rec = work.tile([P, GATES, BATCH], F32, tag="rec_sb", name="rec")
-            nc.scalar.copy(out=rec[:], in_=sums[:])
-            return rec
+            if part == 1:
+                rec[jt] = work.tile([P, GATES, BATCH], F32, tag="rec_sb", name="rec")
+                nc.scalar.copy(out=rec[jt][:], in_=rec_sums[jt][:])
 
         def transpose_w(jt):
-            grouped = []
+            if jt >= ROW_TILES:
+                return
+            w_grouped[jt] = []
             for n in range(GATES):
                 bank = transpose_words(w_raw[jt][n][:])
                 values = stage.tile([P, 4 * PASSES * P], BF16, tag="w_grouped", name="w_grouped", align_bytes=64)
@@ -177,27 +190,27 @@ def tile_lstm_cell_pa_kernel(
                     out=values[:].bitcast(F32).rearrange("p (c j u) -> p c j u", c=PASSES, u=2),
                     in_=by_pass(bank),
                 )
-                grouped.append(values)
-            return grouped
+                w_grouped[jt].append(values)
 
-        def quantise_w(grouped):
-            w_mx = []
+        def quantise_w(jt):
+            if jt >= ROW_TILES:
+                return
+            w_mx[jt] = []
             for n in range(GATES):
                 codes = stage.tile([P, PASSES, P], U32, tag="w_codes", name="w_codes", align_bytes=64)
                 scales = stage.tile([P, PASSES, P], U8, tag="w_scales", name="w_scales", align_bytes=64)
                 nc.vector.quantize_mx(
                     out=codes[:].rearrange("p c j -> p (c j)").bitcast(FP8X4),
                     scales=scales[:].rearrange("p c j -> p (c j)"),
-                    in_=grouped[n][:],
+                    in_=w_grouped[jt][n][:],
                 )
-                w_mx.append((codes, scales))
-            return w_mx
+                w_mx[jt].append((codes, scales))
 
-        def gates(jt, half, w_mx, rec):
+        def gates(jt, half):
             tokens = slice(half * HALF, (half + 1) * HALF)
             gate_tiles = []
             for n in range(GATES):
-                codes, scales = w_mx[n]
+                codes, scales = w_mx[jt][n]
                 acc = acc_psum.tile([P, HALF_STEPS, BATCH], F32, tag="acc", name="acc")
                 for c in range(PASSES):
                     nc.tensor.matmul_mx(
@@ -213,28 +226,29 @@ def tile_lstm_cell_pa_kernel(
                 nc.vector.tensor_tensor(
                     out=gate[:],
                     in0=acc[:],
-                    in1=rec[:, n, :].unsqueeze(1).to_broadcast([P, HALF_STEPS, BATCH]),
+                    in1=rec[jt][:, n, :].unsqueeze(1).to_broadcast([P, HALF_STEPS, BATCH]),
                     op=ALU.add,
                 )
                 nc.scalar.activation(out=gate[:], in_=gate[:], func=gate_func[n], bias=bias[:, n, jt : jt + 1])
                 gate_tiles.append(gate)
             return gate_tiles
 
-        def products(engine, jt, gate_tiles):
+        def cell(jt, half, gate_tiles):
             f_gate, i_gate, g_gate = gate_tiles
-            engine.tensor_tensor(
+            nc.vector.tensor_tensor(
                 out=f_gate[:],
                 in0=f_gate[:],
                 in1=c0T[:, jt, :].unsqueeze(1).to_broadcast([P, HALF_STEPS, BATCH]),
                 op=ALU.mult,
             )
+            engine = nc.vector if jt == ROW_TILES - 1 else nc.gpsimd
             engine.tensor_tensor(out=i_gate[:], in0=i_gate[:], in1=g_gate[:], op=ALU.mult)
+            c_new = (keep if half == 1 else work).tile([P, HALF_STEPS, BATCH], F32, tag="c_new", name="c_new")
+            engine.tensor_tensor(out=c_new[:], in0=f_gate[:], in1=i_gate[:], op=ALU.add)
+            return c_new
 
-        def finish(jt, half, gate_tiles):
-            pool = keep if half == 1 else work
-            c_new = pool.tile([P, HALF_STEPS, BATCH], F32, tag="c_new", name="c_new")
-            nc.vector.tensor_tensor(out=c_new[:], in0=gate_tiles[0][:], in1=gate_tiles[1][:], op=ALU.add)
-            h_new = pool.tile([P, HALF_STEPS, BATCH], F32, tag="h_new", name="h_new")
+        def finish(jt, half, c_new):
+            h_new = (keep if half == 1 else work).tile([P, HALF_STEPS, BATCH], F32, tag="h_new", name="h_new")
             nc.scalar.activation(out=h_new[:], in_=c_new[:], func=ACT.Tanh)
             nc.sync.dma_start(
                 out=out_0[jt * P : (jt + 1) * P, half * HALF : (half + 1) * HALF],
@@ -257,12 +271,11 @@ def tile_lstm_cell_pa_kernel(
 
         prepare_x(1)
         prepare_h0()
-        r_T = transpose_r(0)
-        w_grouped = transpose_w(0)
-        rec_sums = rec_psum.tile([P, GATES, BATCH], F32, tag="rec", name="rec_sums")
-        recurrent_matmuls(rec_sums, r_T, rec_steps)
-        rec = recurrent_out(rec_sums)
-        w_mx = quantise_w(w_grouped)
+        transpose_r(0)
+        transpose_w(0)
+        recurrent_matmuls(0, 0)
+        transpose_r(1)
+        quantise_w(0)
 
         bias_psum = flip_psum.tile([P, P], BF16, tag="flip", name="bias_psum")
         nc.tensor.transpose(bias_psum[:], bias_rows[:], ident_bf16[:])
@@ -274,43 +287,37 @@ def tile_lstm_cell_pa_kernel(
         bias = const.tile([P, GATES, ROW_TILES], F32)
         nc.vector.tensor_tensor(out=bias[:], in0=bias_pairs[:, :, 0, :], in1=bias_pairs[:, :, 1, :], op=ALU.add)
 
-        c0_psum = flip_psum.tile([P, ROW_TILES, BATCH], BF16, tag="flip", name="c0_psum")
+        c0T = c0_psum.tile([P, ROW_TILES, BATCH], BF16, tag="c0T", name="c0T")
         for jt in range(ROW_TILES):
-            nc.tensor.transpose(c0_psum[:, jt, :], c0_raw[:, jt * P : (jt + 1) * P], ident_bf16[:])
-        c0T = const.tile([P, ROW_TILES, BATCH], F32)
-        nc.scalar.copy(out=c0T[:], in_=c0_psum[:])
+            nc.tensor.transpose(c0T[:, jt, :], c0_raw[:, jt * P : (jt + 1) * P], ident_bf16[:])
 
         prepare_x(0)
-        r_T_next = transpose_r(1)
+        recurrent_matmuls(0, 1)
+        transpose_w(1)
 
-        unfinished = None
+        gated = None
+        updated = None
         for jt in range(ROW_TILES):
             if jt + LOAD_AHEAD < ROW_TILES:
                 load_row_tile(jt + LOAD_AHEAD)
-            more = jt + 1 < ROW_TILES
             for half in (1, 0):
-                gate_tiles = gates(jt, half, w_mx, rec)
-                if half == 1 and more:
-                    w_grouped = transpose_w(jt + 1)
-                    rec_sums = rec_psum.tile([P, GATES, BATCH], F32, tag="rec", name="rec_sums")
-                    recurrent_matmuls(rec_sums, r_T_next, rec_steps[: len(rec_steps) // 2])
-                if half == 0 and more:
-                    r_T = r_T_next
-                    if jt + 2 < ROW_TILES:
-                        r_T_next = transpose_r(jt + 2)
-                    recurrent_matmuls(rec_sums, r_T, rec_steps[len(rec_steps) // 2 :])
-                    rec_next = recurrent_out(rec_sums)
-                if unfinished is not None:
-                    finish(*unfinished)
-                very_last = jt == ROW_TILES - 1 and half == 0
-                products(nc.vector if very_last else nc.gpsimd, jt, gate_tiles)
-                unfinished = (jt, half, gate_tiles)
-                if half == 1 and more:
-                    w_mx_next = quantise_w(w_grouped)
-            if more:
-                w_mx = w_mx_next
-                rec = rec_next
-            if jt == WORD_BLOCKS:
+                gate_tiles = gates(jt, half)
+                if half == 1:
+                    quantise_w(jt + 1)
+                before = updated
+                if gated is not None:
+                    updated = (gated[0], gated[1], cell(*gated))
+                gated = (jt, half, gate_tiles)
+                if half == 1:
+                    recurrent_matmuls(jt + 1, 0)
+                    transpose_r(jt + 2)
+                else:
+                    recurrent_matmuls(jt + 1, 1)
+                    transpose_w(jt + 2)
+                if before is not None:
+                    finish(*before)
+            if jt == ROW_TILES - 2:
                 store_last(0)
+        finish(*updated)
+        finish(gated[0], gated[1], cell(*gated))
         store_last(WORD_BLOCKS)
-        finish(*unfinished)

@@ -77,25 +77,34 @@ def tile_lstm_cell_pa_kernel(
             nc.sync.dma_start(out=raw[:], in_=matrix[jt * P : (jt + 1) * P, :])
             return raw
 
-        def load_row_tile(jt):
+        def load_r(jt):
             r_raw[jt] = [load_rows(r_dram[n], jt, "r_raw") for n in range(GATES)]
+
+        def load_w(jt):
             w_raw[jt] = [load_rows(w_dram[n], jt, "w_raw") for n in range(GATES)]
 
         r_raw = {}
         w_raw = {}
+        nc.sync.dma_start(out=h0_raw[:], in_=h0)
+        load_r(0)
         load_x(4)
         load_x(6)
-        nc.sync.dma_start(out=h0_raw[:], in_=h0)
-        load_row_tile(0)
+        load_w(0)
         nc.sync.dma_start(out=c0_raw[:], in_=c0)
+        load_r(1)
         load_x(0)
         load_x(2)
-        for jt in range(1, LOAD_AHEAD):
-            load_row_tile(jt)
+        load_w(1)
+        for jt in range(2, LOAD_AHEAD):
+            load_r(jt)
+            load_w(jt)
 
-        def transpose_words(rows_bf16):
+        def transpose_words(rows_bf16, borrow=False):
             words = rows_bf16.bitcast(F32)
-            bank = flip_psum.tile([P, WORD_BLOCKS, P], F32, tag="flip", name="bank")
+            if borrow:
+                bank = acc_psum.tile([P, WORD_BLOCKS, P], F32, tag="acc", name="bank")
+            else:
+                bank = flip_psum.tile([P, WORD_BLOCKS, P], F32, tag="flip", name="bank")
             for q in range(WORD_BLOCKS):
                 nc.tensor.transpose(bank[:, q, :], words[:, q * P : (q + 1) * P], ident_f32[:])
             return bank
@@ -116,7 +125,7 @@ def tile_lstm_cell_pa_kernel(
 
         def prepare_x(half):
             for t in range(half * HALF_STEPS, (half + 1) * HALF_STEPS):
-                bank = transpose_words(x_raw[:, t, :])
+                bank = transpose_words(x_raw[:, t, :], borrow=(t % 2 == 1))
                 columns = x_grouped_words[:, :, t * BATCH : (t + 1) * BATCH, :]
                 if t % 2 == 0:
                     nc.scalar.copy(out=columns, in_=by_pass(bank))
@@ -144,15 +153,14 @@ def tile_lstm_cell_pa_kernel(
         w_grouped = {}
         w_mx = {}
 
-        def transpose_r(jt):
+        def transpose_r(jt, prologue=False):
             if jt >= ROW_TILES:
                 return
             r_T[jt] = []
             for n in range(GATES):
-                bank = transpose_words(r_raw[jt][n][:])
+                bank = transpose_words(r_raw[jt][n][:], borrow=(prologue and n % 2 == 1))
                 flipped = stage.tile([P, WORD_BLOCKS, P, 2], BF16, tag="r_T", name="r_T")
-                leave_psum(
-                    n,
+                nc.scalar.copy(
                     out=flipped[:].rearrange("p q j e -> p (q j e)").bitcast(F32),
                     in_=bank[:].rearrange("p q j -> p (q j)"),
                 )
@@ -176,14 +184,14 @@ def tile_lstm_cell_pa_kernel(
                 )
             if part == 1:
                 rec[jt] = work.tile([P, GATES, BATCH], F32, tag="rec_sb", name="rec")
-                nc.scalar.copy(out=rec[jt][:], in_=rec_sums[jt][:])
+                nc.vector.tensor_copy(out=rec[jt][:], in_=rec_sums[jt][:])
 
-        def transpose_w(jt):
+        def transpose_w(jt, prologue=False):
             if jt >= ROW_TILES:
                 return
             w_grouped[jt] = []
             for n in range(GATES):
-                bank = transpose_words(w_raw[jt][n][:])
+                bank = transpose_words(w_raw[jt][n][:], borrow=(prologue and n % 2 == 1))
                 values = stage.tile([P, 4 * PASSES * P], BF16, tag="w_grouped", name="w_grouped", align_bytes=64)
                 leave_psum(
                     n,
@@ -269,13 +277,12 @@ def tile_lstm_cell_pa_kernel(
                 leave_psum(which, out=last_sb[:, which, columns], in_=bank[:].rearrange("p q j -> p (q j)"))
                 nc.sync.dma_start(out=out_last[:, columns], in_=last_sb[:, which, columns])
 
-        prepare_x(1)
         prepare_h0()
-        transpose_r(0)
-        transpose_w(0)
+        transpose_r(0, prologue=True)
+        prepare_x(1)
         recurrent_matmuls(0, 0)
-        transpose_r(1)
-        quantise_w(0)
+        recurrent_matmuls(0, 1)
+        transpose_w(0, prologue=True)
 
         bias_psum = flip_psum.tile([P, P], BF16, tag="flip", name="bias_psum")
         nc.tensor.transpose(bias_psum[:], bias_rows[:], ident_bf16[:])
@@ -291,15 +298,17 @@ def tile_lstm_cell_pa_kernel(
         for jt in range(ROW_TILES):
             nc.tensor.transpose(c0T[:, jt, :], c0_raw[:, jt * P : (jt + 1) * P], ident_bf16[:])
 
+        quantise_w(0)
+        transpose_r(1, prologue=True)
         prepare_x(0)
-        recurrent_matmuls(0, 1)
-        transpose_w(1)
+        transpose_w(1, prologue=True)
 
         gated = None
         updated = None
         for jt in range(ROW_TILES):
             if jt + LOAD_AHEAD < ROW_TILES:
-                load_row_tile(jt + LOAD_AHEAD)
+                load_r(jt + LOAD_AHEAD)
+                load_w(jt + LOAD_AHEAD)
             for half in (1, 0):
                 gate_tiles = gates(jt, half)
                 if half == 1:

@@ -20,7 +20,7 @@ PASSES = FEATURES // (4 * P)
 HALF_STEPS = STEPS // 2
 HALF = HALF_STEPS * BATCH
 TOKENS = STEPS * BATCH
-LOAD_AHEAD = 3
+LOAD_AHEAD = 4
 
 FLOPS = 2 * TOKENS * FEATURES * HIDDEN * GATES + 2 * BATCH * HIDDEN * HIDDEN * GATES
 
@@ -241,14 +241,17 @@ def tile_lstm_cell_pa_kernel(
                 gate_tiles.append(gate)
             return gate_tiles
 
-        def cell(jt, half, gate_tiles):
-            f_gate, i_gate, g_gate = gate_tiles
+        def kept_state(jt, half, gate_tiles):
+            f_gate = gate_tiles[0]
             nc.vector.tensor_tensor(
                 out=f_gate[:],
                 in0=f_gate[:],
                 in1=c0T[:, jt, :].unsqueeze(1).to_broadcast([P, HALF_STEPS, BATCH]),
                 op=ALU.mult,
             )
+
+        def new_state(jt, half, gate_tiles):
+            f_gate, i_gate, g_gate = gate_tiles
             engine = nc.vector if jt == ROW_TILES - 1 else nc.gpsimd
             engine.tensor_tensor(out=i_gate[:], in0=i_gate[:], in1=g_gate[:], op=ALU.mult)
             c_new = (keep if half == 1 else work).tile([P, HALF_STEPS, BATCH], F32, tag="c_new", name="c_new")
@@ -311,11 +314,13 @@ def tile_lstm_cell_pa_kernel(
                 load_w(jt + LOAD_AHEAD)
             for half in (1, 0):
                 gate_tiles = gates(jt, half)
-                if half == 1:
-                    quantise_w(jt + 1)
                 before = updated
                 if gated is not None:
-                    updated = (gated[0], gated[1], cell(*gated))
+                    kept_state(*gated)
+                if half == 1:
+                    quantise_w(jt + 1)
+                if gated is not None:
+                    updated = (gated[0], gated[1], new_state(*gated))
                 gated = (jt, half, gate_tiles)
                 if half == 1:
                     recurrent_matmuls(jt + 1, 0)
@@ -328,5 +333,6 @@ def tile_lstm_cell_pa_kernel(
             if jt == ROW_TILES - 2:
                 store_last(0)
         finish(*updated)
-        finish(gated[0], gated[1], cell(*gated))
+        kept_state(*gated)
+        finish(gated[0], gated[1], new_state(*gated))
         store_last(WORD_BLOCKS)

from contextlib import ExitStack

import concourse.mybir as mybir
from concourse.masks import make_identity

F32 = mybir.dt.float32
BF16 = mybir.dt.bfloat16
U32 = mybir.dt.uint32
U8 = mybir.dt.uint8
FP8X4 = mybir.dt.float8_e4m3fn_x4
ACT = mybir.ActivationFunctionType
ALU = mybir.AluOpType

P = 128
BATCH, STEPS, FEATURES, HIDDEN = 128, 8, 1024, 1024
GATES = 3
ROW_TILES = HIDDEN // P
WORD_BLOCKS = FEATURES // (2 * P)
PASSES = FEATURES // (4 * P)
HALF_STEPS = STEPS // 2
HALF = HALF_STEPS * BATCH
TOKENS = STEPS * BATCH
LOAD_AHEAD = 4

FLOPS = 2 * TOKENS * FEATURES * HIDDEN * GATES + 2 * BATCH * HIDDEN * HIDDEN * GATES


def tile_lstm_cell_pa_kernel(
    tc, x, h0, c0, W_f, b_f, R_f, rb_f, W_i, b_i, R_i, rb_i, W_g, b_g, R_g, rb_g, out_0, out_1, out_2
):
    nc = tc.nc
    w_dram = (W_f, W_i, W_g)
    r_dram = (R_f, R_i, R_g)
    bias_dram = (b_f, rb_f, b_i, rb_i, b_g, rb_g)
    gate_func = (ACT.Sigmoid, ACT.Sigmoid, ACT.Tanh)

    with ExitStack() as ctx:
        const = ctx.enter_context(tc.tile_pool(name="const", bufs=1))
        raw_pool = ctx.enter_context(tc.tile_pool(name="raw", bufs=2 * GATES * LOAD_AHEAD))
        stage = ctx.enter_context(tc.tile_pool(name="stage", bufs=6))
        work = ctx.enter_context(tc.tile_pool(name="work", bufs=3))
        keep = ctx.enter_context(tc.tile_pool(name="keep", bufs=ROW_TILES))
        flip_psum = ctx.enter_context(tc.psum_pool(name="flip_psum", bufs=3))
        rec_psum = ctx.enter_context(tc.psum_pool(name="rec_psum", bufs=1))
        acc_psum = ctx.enter_context(tc.psum_pool(name="acc_psum", bufs=GATES))
        c0_psum = ctx.enter_context(tc.psum_pool(name="c0_psum", bufs=1))

        ctx.enter_context(tc.manual_schedule())

        ident_f32 = const.tile([P, P], F32)
        make_identity(nc, ident_f32[:])
        ident_bf16 = const.tile([P, P], BF16)
        make_identity(nc, ident_bf16[:])

        bias_rows = const.tile([P, P], BF16)
        nc.vector.memset(bias_rows[:], 0.0)
        for v, vector in enumerate(bias_dram):
            nc.scalar.dma_start(
                out=bias_rows[v * ROW_TILES : (v + 1) * ROW_TILES, :],
                in_=vector.rearrange("(jt p) -> jt p", p=P),
            )

        table_warmer = const.tile([P, 1], F32)
        nc.vector.memset(table_warmer[:], 0.0)
        nc.scalar.activation(out=table_warmer[:], in_=table_warmer[:], func=ACT.Sigmoid)

        x_raw = const.tile([P, STEPS, FEATURES], BF16)
        h0_raw = const.tile([P, HIDDEN], BF16)
        c0_raw = const.tile([P, HIDDEN], BF16)

        def load_x(first_step):
            steps = slice(first_step, first_step + 2)
            nc.sync.dma_start(out=x_raw[:, steps, :], in_=x[:, steps, :])

        def load_rows(matrix, jt, name):
            raw = raw_pool.tile([P, FEATURES], BF16, tag="raw", name=name)
            nc.sync.dma_start(out=raw[:], in_=matrix[jt * P : (jt + 1) * P, :])
            return raw

        def load_r(jt):
            r_raw[jt] = [load_rows(r_dram[n], jt, "r_raw") for n in range(GATES)]

        def load_w(jt):
            w_raw[jt] = [load_rows(w_dram[n], jt, "w_raw") for n in range(GATES)]

        r_raw = {}
        w_raw = {}
        nc.sync.dma_start(out=h0_raw[:], in_=h0)
        load_r(0)
        load_x(4)
        load_x(6)
        load_w(0)
        nc.sync.dma_start(out=c0_raw[:], in_=c0)
        load_r(1)
        load_x(0)
        load_x(2)
        load_w(1)
        for jt in range(2, LOAD_AHEAD):
            load_r(jt)
            load_w(jt)

        def transpose_words(rows_bf16, borrow=False):
            words = rows_bf16.bitcast(F32)
            if borrow:
                bank = acc_psum.tile([P, WORD_BLOCKS, P], F32, tag="acc", name="bank")
            else:
                bank = flip_psum.tile([P, WORD_BLOCKS, P], F32, tag="flip", name="bank")
            for q in range(WORD_BLOCKS):
                nc.tensor.transpose(bank[:, q, :], words[:, q * P : (q + 1) * P], ident_f32[:])
            return bank

        def by_pass(bank):
            return bank[:].rearrange("p (c u) n -> p c n u", u=2)

        def leave_psum(n, out, in_):
            if n % GATES == 1:
                nc.vector.tensor_copy(out=out, in_=in_)
            else:
                nc.scalar.copy(out=out, in_=in_)

        x_grouped = const.tile([P, PASSES, 4 * TOKENS], BF16, align_bytes=64)
        x_codes = const.tile([P, PASSES, TOKENS], U32, align_bytes=64)
        x_scales = const.tile([P, PASSES, TOKENS], U8, align_bytes=64)
        x_grouped_words = x_grouped[:].bitcast(F32).rearrange("p c (n u) -> p c n u", u=2)

        def prepare_x(half):
            for t in range(half * HALF_STEPS, (half + 1) * HALF_STEPS):
                bank = transpose_words(x_raw[:, t, :], borrow=(t % 2 == 1))
                columns = x_grouped_words[:, :, t * BATCH : (t + 1) * BATCH, :]
                if t % 2 == 0:
                    nc.scalar.copy(out=columns, in_=by_pass(bank))
                else:
                    nc.vector.tensor_copy(out=columns, in_=by_pass(bank))
            for c in range(PASSES):
                nc.vector.quantize_mx(
                    out=x_codes[:, c, half * HALF : (half + 1) * HALF].bitcast(FP8X4),
                    scales=x_scales[:, c, half * HALF : (half + 1) * HALF],
                    in_=x_grouped[:, c, half * 4 * HALF : (half + 1) * 4 * HALF],
                )

        h0T = const.tile([P, WORD_BLOCKS, BATCH, 2], BF16)

        def prepare_h0():
            bank = transpose_words(h0_raw[:])
            nc.vector.tensor_copy(
                out=h0T[:].rearrange("p q b e -> p (q b e)").bitcast(F32),
                in_=bank[:].rearrange("p q b -> p (q b)"),
            )

        r_T = {}
        rec_sums = {}
        rec = {}
        w_grouped = {}
        w_mx = {}

        def transpose_r(jt, prologue=False):
            if jt >= ROW_TILES:
                return
            r_T[jt] = []
            for n in range(GATES):
                bank = transpose_words(r_raw[jt][n][:], borrow=(prologue and n % 2 == 1))
                flipped = stage.tile([P, WORD_BLOCKS, P, 2], BF16, tag="r_T", name="r_T")
                nc.scalar.copy(
                    out=flipped[:].rearrange("p q j e -> p (q j e)").bitcast(F32),
                    in_=bank[:].rearrange("p q j -> p (q j)"),
                )
                r_T[jt].append(flipped)

        rec_steps = [(n, q, e) for n in range(GATES) for q in range(WORD_BLOCKS) for e in range(2)]

        def recurrent_matmuls(jt, part):
            if jt >= ROW_TILES:
                return
            if part == 0:
                rec_sums[jt] = rec_psum.tile([P, GATES, BATCH], F32, tag="rec", name="rec_sums")
            count = len(rec_steps) // 2
            for n, q, e in rec_steps[part * count : (part + 1) * count]:
                nc.tensor.matmul(
                    out=rec_sums[jt][:, n, :],
                    lhsT=r_T[jt][n][:, q, :, e],
                    rhs=h0T[:, q, :, e],
                    start=(q == 0 and e == 0),
                    stop=(q == WORD_BLOCKS - 1 and e == 1),
                )
            if part == 1:
                rec[jt] = work.tile([P, GATES, BATCH], F32, tag="rec_sb", name="rec")
                nc.vector.tensor_copy(out=rec[jt][:], in_=rec_sums[jt][:])

        def transpose_w(jt, prologue=False):
            if jt >= ROW_TILES:
                return
            w_grouped[jt] = []
            for n in range(GATES):
                bank = transpose_words(w_raw[jt][n][:], borrow=(prologue and n % 2 == 1))
                values = stage.tile([P, 4 * PASSES * P], BF16, tag="w_grouped", name="w_grouped", align_bytes=64)
                leave_psum(
                    n,
                    out=values[:].bitcast(F32).rearrange("p (c j u) -> p c j u", c=PASSES, u=2),
                    in_=by_pass(bank),
                )
                w_grouped[jt].append(values)

        def quantise_w(jt):
            if jt >= ROW_TILES:
                return
            w_mx[jt] = []
            for n in range(GATES):
                codes = stage.tile([P, PASSES, P], U32, tag="w_codes", name="w_codes", align_bytes=64)
                scales = stage.tile([P, PASSES, P], U8, tag="w_scales", name="w_scales", align_bytes=64)
                nc.vector.quantize_mx(
                    out=codes[:].rearrange("p c j -> p (c j)").bitcast(FP8X4),
                    scales=scales[:].rearrange("p c j -> p (c j)"),
                    in_=w_grouped[jt][n][:],
                )
                w_mx[jt].append((codes, scales))

        def gates(jt, half):
            tokens = slice(half * HALF, (half + 1) * HALF)
            gate_tiles = []
            for n in range(GATES):
                codes, scales = w_mx[jt][n]
                acc = acc_psum.tile([P, HALF_STEPS, BATCH], F32, tag="acc", name="acc")
                for c in range(PASSES):
                    nc.tensor.matmul_mx(
                        out=acc[:].rearrange("p t b -> p (t b)"),
                        lhsT=codes[:, c, :].bitcast(FP8X4),
                        lhsT_scale=scales[:, c, :],
                        rhs=x_codes[:, c, tokens].bitcast(FP8X4),
                        rhs_scale=x_scales[:, c, tokens],
                        start=(c == 0),
                        stop=(c == PASSES - 1),
                    )
                gate = work.tile([P, HALF_STEPS, BATCH], F32, tag="gate%d" % n, name="gate")
                nc.vector.tensor_tensor(
                    out=gate[:],
                    in0=acc[:],
                    in1=rec[jt][:, n, :].unsqueeze(1).to_broadcast([P, HALF_STEPS, BATCH]),
                    op=ALU.add,
                )
                nc.scalar.activation(out=gate[:], in_=gate[:], func=gate_func[n], bias=bias[:, n, jt : jt + 1])
                gate_tiles.append(gate)
            return gate_tiles

        def kept_state(jt, half, gate_tiles):
            f_gate = gate_tiles[0]
            nc.vector.tensor_tensor(
                out=f_gate[:],
                in0=f_gate[:],
                in1=c0T[:, jt, :].unsqueeze(1).to_broadcast([P, HALF_STEPS, BATCH]),
                op=ALU.mult,
            )

        def new_state(jt, half, gate_tiles):
            f_gate, i_gate, g_gate = gate_tiles
            engine = nc.vector if jt == ROW_TILES - 1 else nc.gpsimd
            engine.tensor_tensor(out=i_gate[:], in0=i_gate[:], in1=g_gate[:], op=ALU.mult)
            c_new = (keep if half == 1 else work).tile([P, HALF_STEPS, BATCH], F32, tag="c_new", name="c_new")
            engine.tensor_tensor(out=c_new[:], in0=f_gate[:], in1=i_gate[:], op=ALU.add)
            return c_new

        def finish(jt, half, c_new):
            h_new = (keep if half == 1 else work).tile([P, HALF_STEPS, BATCH], F32, tag="h_new", name="h_new")
            nc.scalar.activation(out=h_new[:], in_=c_new[:], func=ACT.Tanh)
            nc.sync.dma_start(
                out=out_0[jt * P : (jt + 1) * P, half * HALF : (half + 1) * HALF],
                in_=h_new[:].rearrange("p t b -> p (t b)"),
            )
            if half == 1:
                last_tiles[jt] = (h_new, c_new)

        last_tiles = {}
        last_sb = const.tile([P, 2, HIDDEN], F32)

        def store_last(first):
            columns = slice(first * P, (first + WORD_BLOCKS) * P)
            for which, out_last in enumerate((out_1, out_2)):
                bank = flip_psum.tile([P, WORD_BLOCKS, P], F32, tag="flip", name="last_bank")
                for q in range(WORD_BLOCKS):
                    nc.tensor.transpose(bank[:, q, :], last_tiles[first + q][which][:, HALF_STEPS - 1, :], ident_f32[:])
                leave_psum(which, out=last_sb[:, which, columns], in_=bank[:].rearrange("p q j -> p (q j)"))
                nc.sync.dma_start(out=out_last[:, columns], in_=last_sb[:, which, columns])

        prepare_h0()
        transpose_r(0, prologue=True)
        prepare_x(1)
        recurrent_matmuls(0, 0)
        recurrent_matmuls(0, 1)
        transpose_w(0, prologue=True)

        bias_psum = flip_psum.tile([P, P], BF16, tag="flip", name="bias_psum")
        nc.tensor.transpose(bias_psum[:], bias_rows[:], ident_bf16[:])
        bias_pairs = const.tile([P, GATES, 2, ROW_TILES], F32)
        nc.vector.tensor_copy(
            out=bias_pairs[:],
            in_=bias_psum[:, 0 : 2 * GATES * ROW_TILES].rearrange("p (n s jt) -> p n s jt", n=GATES, s=2),
        )
        bias = const.tile([P, GATES, ROW_TILES], F32)
        nc.vector.tensor_tensor(out=bias[:], in0=bias_pairs[:, :, 0, :], in1=bias_pairs[:, :, 1, :], op=ALU.add)

        c0T = c0_psum.tile([P, ROW_TILES, BATCH], BF16, tag="c0T", name="c0T")
        for jt in range(ROW_TILES):
            nc.tensor.transpose(c0T[:, jt, :], c0_raw[:, jt * P : (jt + 1) * P], ident_bf16[:])

        quantise_w(0)
        transpose_r(1, prologue=True)
        prepare_x(0)
        transpose_w(1, prologue=True)

        gated = None
        updated = None
        for jt in range(ROW_TILES):
            if jt + LOAD_AHEAD < ROW_TILES:
                load_r(jt + LOAD_AHEAD)
                load_w(jt + LOAD_AHEAD)
            for half in (1, 0):
                gate_tiles = gates(jt, half)
                before = updated
                if gated is not None:
                    kept_state(*gated)
                if half == 1:
                    quantise_w(jt + 1)
                if gated is not None:
                    updated = (gated[0], gated[1], new_state(*gated))
                gated = (jt, half, gate_tiles)
                if half == 1:
                    recurrent_matmuls(jt + 1, 0)
                    transpose_r(jt + 2)
                else:
                    recurrent_matmuls(jt + 1, 1)
                    transpose_w(jt + 2)
                if before is not None:
                    finish(*before)
            if jt == ROW_TILES - 2:
                store_last(0)
        finish(*updated)
        kept_state(*gated)
        finish(gated[0], gated[1], new_state(*gated))
        store_last(WORD_BLOCKS)
